import numpy as np
import ml_dtypes


def mxq(x, axis, fmt="e4m3"):
    dtype, down = {"e4m3": (ml_dtypes.float8_e4m3fn, 7), "e5m2": (ml_dtypes.float8_e5m2, 14)}[fmt]
    v = np.moveaxis(np.asarray(x, np.float32).astype(ml_dtypes.bfloat16).astype(np.float64), axis, -1)
    blocks = v.reshape(v.shape[:-1] + (-1, 32))
    amax = np.abs(blocks).max(-1, keepdims=True)
    byte = np.maximum(np.where(amax > 0, np.frexp(amax)[1] - 1 + 127, 0) - down, 1)
    scale = np.exp2(byte - 127.0)
    codes = (blocks / scale).astype(np.float32).astype(dtype).astype(np.float64)
    return np.moveaxis((codes * scale).reshape(v.shape), -1, axis)


WIDE = False


def mx_kscale(k):
    if not WIDE:
        return np.ones(k)
    levels = np.array([10, -10, 5, -5, 0])
    if k % 512:
        return np.exp2(np.random.permutation(np.resize(levels, k // 32))).repeat(32)
    a = np.empty((k // 512, 16))
    for p in range(k // 512):
        a[p, :8] = np.random.permutation(np.resize(levels, 8))
        for g in range(8):
            far = levels[np.abs(levels - a[p, g]) >= 10]
            a[p, g + 8] = far[np.random.randint(len(far))]
    return np.exp2(a.ravel()).repeat(32)


BF16 = ml_dtypes.bfloat16


def bf(x):
    return np.asarray(x, np.float32).astype(BF16)


def f64(x):
    return np.asarray(x).astype(np.float64)


B, I, C, K, L, S0, S1, S2, S3, S4 = 2, 8, 512, 7, 5, 16, 12, 8, 6, 4
P = S2 * S2


def setup_inputs():
    t = mx_kscale(C)
    return {"q": bf(np.random.standard_normal((B, I, C))),
            "feats": bf(np.random.standard_normal((B, C, S2, S2)) * t[:, None, None]),
            "po_w": bf(np.random.standard_normal((C, C)) / np.sqrt(C) / t),
            "po_b": bf(np.random.standard_normal(C) * 0.3)}


def reference(q, feats, po_w, po_b):
    m = f64(q)[:, :, :, None] * f64(feats).reshape(B, C, P)[:, None]
    o = (mxq(f64(po_w), 1, "e4m3") @ mxq(m, 2, "e4m3")) + f64(po_b)[:, None]
    return o.reshape(B, I, C, S2, S2)

@@ -1,0 +1,171 @@
+from contextlib import ExitStack
+
+import concourse.mybir as mybir
+from concourse.masks import make_identity
+
+F32 = mybir.dt.float32
+BF16 = mybir.dt.bfloat16
+U32 = mybir.dt.uint32
+U8 = mybir.dt.uint8
+FP8X4 = mybir.dt.float8_e4m3fn_x4
+
+P = 128
+PACK = 4
+HALVES = 2
+
+IMAGES = 2
+INSTANCES = 8
+CHANNELS = 512
+PIXELS = 64
+ROWS = IMAGES * INSTANCES
+O_TILES = CHANNELS // P
+GROUP = 4
+GROUPS = ROWS // GROUP
+GROUP_COLS = GROUP * PIXELS
+SHARED_FROM = 2
+
+FLOPS = 2 * ROWS * PIXELS * CHANNELS * CHANNELS
+
+
+def tile_rpn_modulator_pb_s_kernel(tc, q, feats, po_w, po_b, out):
+    nc = tc.nc
+    with ExitStack() as ctx:
+        consts = ctx.enter_context(tc.tile_pool(name="consts", bufs=1))
+        weights = ctx.enter_context(tc.tile_pool(name="weights", bufs=O_TILES))
+        columns = ctx.enter_context(tc.tile_pool(name="columns", bufs=GROUPS))
+        turned = ctx.enter_context(tc.psum_pool(name="turned", bufs=4))
+        sums = ctx.enter_context(tc.psum_pool(name="sums", bufs=4))
+        ctx.enter_context(tc.manual_schedule())
+
+        identity = consts.tile([P, P], F32)
+        make_identity(nc, identity[:])
+
+        q_rows = consts.tile([P, CHANNELS], BF16)
+        for k in range(2):
+            nc.sync.dma_start(
+                out=q_rows[k * ROWS : (k + 1) * ROWS, :], in_=q.rearrange("b i c -> (b i) c")
+            )
+        nc.vector.memset(q_rows[2 * ROWS : 4 * ROWS, :], 0.0)
+        nc.vector.memset(q_rows[4 * ROWS : P, :], 0.0)
+        feats_rows = consts.tile([P, IMAGES, PACK * PIXELS], BF16)
+        nc.sync.dma_start(
+            out=feats_rows[:], in_=feats.rearrange("b (p j) y x -> p b (j y x)", j=PACK)
+        )
+        w_view = po_w.rearrange("(m t) c -> m t c", t=O_TILES)
+        w_rows_all = []
+        for t in range(O_TILES):
+            w_rows = weights.tile([P, CHANNELS], BF16)
+            nc.sync.dma_start(out=w_rows[:], in_=w_view[:, t, :])
+            w_rows_all.append(w_rows)
+        bias_bf16 = consts.tile([P, O_TILES], BF16)
+        nc.sync.dma_start(out=bias_bf16[:], in_=po_b.rearrange("(m t) -> m t", t=O_TILES))
+        bias = consts.tile([P, O_TILES], F32)
+        nc.gpsimd.tensor_copy(out=bias[:], in_=bias_bf16[:])
+
+        feats_grouped = consts.tile([P, IMAGES, PIXELS, PACK], BF16)
+        nc.vector.tensor_copy(
+            out=feats_grouped[:], in_=feats_rows[:].rearrange("p b (j w) -> p b w j", j=PACK)
+        )
+
+        def turn(rows):
+            words = rows[:].bitcast(F32).rearrange("r (p u) -> r u p", u=HALVES)
+            halves = turned.tile([P, HALVES, P], F32)
+            for u in range(HALVES):
+                nc.tensor.transpose(halves[:, u, :], words[:, u, :], identity[:])
+            return halves
+
+        def turn_q():
+            q_turned = turn(q_rows)
+            q_cols = consts.tile([P, ROWS, PACK], BF16)
+            nc.vector.tensor_copy(
+                out=q_cols[:].rearrange("p r j -> p (r j)").bitcast(F32).rearrange(
+                    "p (r u) -> p r u", u=HALVES
+                ),
+                in_=q_turned[:, :, 0:ROWS].rearrange("p u r -> p r u"),
+            )
+            return q_cols
+
+        def multiply_q(q_cols, g):
+            b = g * GROUP // INSTANCES
+            shape = [P, GROUP, PIXELS, PACK]
+            m_grouped = columns.tile(shape, BF16, align_bytes=64)
+            nc.vector.tensor_tensor(
+                out=m_grouped[:],
+                in0=feats_grouped[:, b].unsqueeze(1).to_broadcast(shape),
+                in1=q_cols[:, g * GROUP : (g + 1) * GROUP, :].unsqueeze(2).to_broadcast(shape),
+                op=mybir.AluOpType.mult,
+            )
+            return m_grouped
+
+        def quantise_columns(m_grouped):
+            m_codes = columns.tile([P, GROUP_COLS], U32, align_bytes=64)
+            m_scales = columns.tile([P, GROUP_COLS], U8, align_bytes=64)
+            nc.vector.quantize_mx(
+                out=m_codes[:].bitcast(FP8X4),
+                scales=m_scales[:],
+                in_=m_grouped[:].rearrange("p i w j -> p (i w j)"),
+            )
+            return m_codes, m_scales
+
+        def turn_weights(t):
+            w_turned = turn(w_rows_all[t])
+            w_grouped = weights.tile([P, P * PACK], BF16, align_bytes=64)
+            nc.scalar.copy(
+                out=w_grouped[:].bitcast(F32).rearrange("p (m u) -> p m u", u=HALVES),
+                in_=w_turned[:].rearrange("p u m -> p m u"),
+            )
+            return w_grouped
+
+        def quantise_weights(w_grouped):
+            w_codes = weights.tile([P, P], U32, align_bytes=64)
+            w_scales = weights.tile([P, P], U8, align_bytes=64)
+            nc.vector.quantize_mx(
+                out=w_codes[:].bitcast(FP8X4), scales=w_scales[:], in_=w_grouped[:]
+            )
+            return w_codes, w_scales
+
+        out_view = out.rearrange("b i (m t) y x -> m (b i) (t y x)", t=O_TILES)
+
+        def finish_group(g, w_operands, m_operand):
+            m_codes, m_scales = m_operand
+            result = columns.tile([P, GROUP, O_TILES, PIXELS], F32)
+            for t in range(O_TILES):
+                w_codes, w_scales = w_operands[t]
+                acc = sums.tile([P, GROUP_COLS], F32)
+                nc.tensor.matmul_mx(
+                    out=acc[:],
+                    lhsT=w_codes[:].bitcast(FP8X4),
+                    lhsT_scale=w_scales[:],
+                    rhs=m_codes[:].bitcast(FP8X4),
+                    rhs_scale=m_scales[:],
+                    start=True,
+                    stop=True,
+                )
+                acc_view = acc[:].rearrange("m (i w) -> m i w", w=PIXELS)
+                if g < SHARED_FROM or t % 2 == 0:
+                    nc.scalar.activation(
+                        out=result[:, :, t, :],
+                        in_=acc_view,
+                        func=mybir.ActivationFunctionType.Identity,
+                        bias=bias[:, t : t + 1],
+                        scale=1.0,
+                    )
+                else:
+                    nc.vector.tensor_scalar_add(
+                        out=result[:, :, t, :], in0=acc_view, scalar1=bias[:, t : t + 1]
+                    )
+            nc.sync.dma_start(
+                out=out_view[:, g * GROUP : (g + 1) * GROUP, :],
+                in_=result[:].rearrange("m i t w -> m i (t w)"),
+            )
+
+        q_cols = turn_q()
+        w_grouped_all = [turn_weights(t) for t in range(O_TILES)]
+        m_grouped = multiply_q(q_cols, 0)
+        w_operands = [quantise_weights(w_grouped_all[0])]
+        m_operands = [quantise_columns(m_grouped)]
+        w_operands.extend(quantise_weights(w_grouped_all[t]) for t in range(1, O_TILES))
+        for g in range(1, GROUPS):
+            m_operands.append(quantise_columns(multiply_q(q_cols, g)))
+        for g in range(GROUPS):
+            finish_group(g, w_operands, m_operands[g])

@@ -8,6 +8,7 @@ BF16 = mybir.dt.bfloat16
 U32 = mybir.dt.uint32
 U8 = mybir.dt.uint8
 FP8X4 = mybir.dt.float8_e4m3fn_x4
+IDENTITY = mybir.ActivationFunctionType.Identity
 
 P = 128
 PACK = 4
@@ -19,22 +20,25 @@ CHANNELS = 512
 PIXELS = 64
 ROWS = IMAGES * INSTANCES
 O_TILES = CHANNELS // P
-GROUP = 4
-GROUPS = ROWS // GROUP
-GROUP_COLS = GROUP * PIXELS
-SHARED_FROM = 2
+GROUP_SIZES = (2, 2, 4, 4, 2, 2)
+SHARED_FROM = 3
+HALVED_BEFORE = 1
+BANKS = 8
 
 FLOPS = 2 * ROWS * PIXELS * CHANNELS * CHANNELS
 
 
 def tile_rpn_modulator_pb_s_kernel(tc, q, feats, po_w, po_b, out):
     nc = tc.nc
+    groups = []
+    for size in GROUP_SIZES:
+        groups.append((sum(GROUP_SIZES[: len(groups)]), size))
     with ExitStack() as ctx:
         consts = ctx.enter_context(tc.tile_pool(name="consts", bufs=1))
+        images = ctx.enter_context(tc.tile_pool(name="images", bufs=IMAGES))
         weights = ctx.enter_context(tc.tile_pool(name="weights", bufs=O_TILES))
-        columns = ctx.enter_context(tc.tile_pool(name="columns", bufs=GROUPS))
-        turned = ctx.enter_context(tc.psum_pool(name="turned", bufs=4))
-        sums = ctx.enter_context(tc.psum_pool(name="sums", bufs=4))
+        columns = ctx.enter_context(tc.tile_pool(name="columns", bufs=len(GROUP_SIZES)))
+        psum = ctx.enter_context(tc.psum_pool(name="psum", bufs=BANKS))
         ctx.enter_context(tc.manual_schedule())
 
         identity = consts.tile([P, P], F32)
@@ -47,35 +51,40 @@ def tile_rpn_modulator_pb_s_kernel(tc, q, feats, po_w, po_b, out):
             )
         nc.vector.memset(q_rows[2 * ROWS : 4 * ROWS, :], 0.0)
         nc.vector.memset(q_rows[4 * ROWS : P, :], 0.0)
-        feats_rows = consts.tile([P, IMAGES, PACK * PIXELS], BF16)
-        nc.sync.dma_start(
-            out=feats_rows[:], in_=feats.rearrange("b (p j) y x -> p b (j y x)", j=PACK)
-        )
-        w_view = po_w.rearrange("(m t) c -> m t c", t=O_TILES)
+        feats_view = feats.rearrange("b (p j) y x -> b p (j y x)", j=PACK)
+        feats_rows_all = []
+        for b in range(IMAGES):
+            feats_rows = images.tile([P, PACK * PIXELS], BF16)
+            nc.sync.dma_start(out=feats_rows[:], in_=feats_view[b])
+            feats_rows_all.append(feats_rows)
+        w_view = po_w.rearrange("(m t) c -> t m c", t=O_TILES)
         w_rows_all = []
         for t in range(O_TILES):
             w_rows = weights.tile([P, CHANNELS], BF16)
-            nc.sync.dma_start(out=w_rows[:], in_=w_view[:, t, :])
+            nc.sync.dma_start(out=w_rows[:], in_=w_view[t])
             w_rows_all.append(w_rows)
-        bias_bf16 = consts.tile([P, O_TILES], BF16)
-        nc.sync.dma_start(out=bias_bf16[:], in_=po_b.rearrange("(m t) -> m t", t=O_TILES))
-        bias = consts.tile([P, O_TILES], F32)
-        nc.gpsimd.tensor_copy(out=bias[:], in_=bias_bf16[:])
+        bias = consts.tile([P, O_TILES], BF16)
+        nc.sync.dma_start(out=bias[:], in_=po_b.rearrange("(m t) -> m t", t=O_TILES))
 
-        feats_grouped = consts.tile([P, IMAGES, PIXELS, PACK], BF16)
-        nc.vector.tensor_copy(
-            out=feats_grouped[:], in_=feats_rows[:].rearrange("p b (j w) -> p b w j", j=PACK)
-        )
+        feats_grouped_all = []
+        for b in range(IMAGES):
+            feats_grouped = images.tile([P, PIXELS, PACK], BF16)
+            regroup = nc.vector.tensor_copy if b == 0 else nc.scalar.copy
+            regroup(
+                out=feats_grouped[:],
+                in_=feats_rows_all[b][:].rearrange("p (j w) -> p w j", j=PACK),
+            )
+            feats_grouped_all.append(feats_grouped)
 
         def turn(rows):
-            words = rows[:].bitcast(F32).rearrange("r (p u) -> r u p", u=HALVES)
-            halves = turned.tile([P, HALVES, P], F32)
+            words = rows.bitcast(F32).rearrange("r (p u) -> r u p", u=HALVES)
+            bank = psum.tile([P, HALVES, P], F32)
             for u in range(HALVES):
-                nc.tensor.transpose(halves[:, u, :], words[:, u, :], identity[:])
-            return halves
+                nc.tensor.transpose(bank[:, u, :], words[:, u, :], identity[:])
+            return bank
 
         def turn_q():
-            q_turned = turn(q_rows)
+            q_turned = turn(q_rows[:])
             q_cols = consts.tile([P, ROWS, PACK], BF16)
             nc.vector.tensor_copy(
                 out=q_cols[:].rearrange("p r j -> p (r j)").bitcast(F32).rearrange(
@@ -86,20 +95,21 @@ def tile_rpn_modulator_pb_s_kernel(tc, q, feats, po_w, po_b, out):
             return q_cols
 
         def multiply_q(q_cols, g):
-            b = g * GROUP // INSTANCES
-            shape = [P, GROUP, PIXELS, PACK]
+            first, size = groups[g]
+            shape = [P, size, PIXELS, PACK]
             m_grouped = columns.tile(shape, BF16, align_bytes=64)
             nc.vector.tensor_tensor(
                 out=m_grouped[:],
-                in0=feats_grouped[:, b].unsqueeze(1).to_broadcast(shape),
-                in1=q_cols[:, g * GROUP : (g + 1) * GROUP, :].unsqueeze(2).to_broadcast(shape),
+                in0=feats_grouped_all[first // INSTANCES][:].unsqueeze(1).to_broadcast(shape),
+                in1=q_cols[:, first : first + size, :].unsqueeze(2).to_broadcast(shape),
                 op=mybir.AluOpType.mult,
             )
             return m_grouped
 
-        def quantise_columns(m_grouped):
-            m_codes = columns.tile([P, GROUP_COLS], U32, align_bytes=64)
-            m_scales = columns.tile([P, GROUP_COLS], U8, align_bytes=64)
+        def quantise_columns(m_grouped, g):
+            cols = groups[g][1] * PIXELS
+            m_codes = columns.tile([P, cols], U32, align_bytes=64)
+            m_scales = columns.tile([P, cols], U8, align_bytes=64)
             nc.vector.quantize_mx(
                 out=m_codes[:].bitcast(FP8X4),
                 scales=m_scales[:],
@@ -108,7 +118,7 @@ def tile_rpn_modulator_pb_s_kernel(tc, q, feats, po_w, po_b, out):
             return m_codes, m_scales
 
         def turn_weights(t):
-            w_turned = turn(w_rows_all[t])
+            w_turned = turn(w_rows_all[t][:])
             w_grouped = weights.tile([P, P * PACK], BF16, align_bytes=64)
             nc.scalar.copy(
                 out=w_grouped[:].bitcast(F32).rearrange("p (m u) -> p m u", u=HALVES),
@@ -124,48 +134,78 @@ def tile_rpn_modulator_pb_s_kernel(tc, q, feats, po_w, po_b, out):
             )
             return w_codes, w_scales
 
-        out_view = out.rearrange("b i (m t) y x -> m (b i) (t y x)", t=O_TILES)
+        out_view = out.rearrange("b i (m t) y x -> m (b i) t (y x)", t=O_TILES)
+
+        def multiply_mx(acc, w_operand, m_operand):
+            w_codes, w_scales = w_operand
+            m_codes, m_scales = m_operand
+            nc.tensor.matmul_mx(
+                out=acc,
+                lhsT=w_codes[:].bitcast(FP8X4),
+                lhsT_scale=w_scales[:],
+                rhs=m_codes[:].bitcast(FP8X4),
+                rhs_scale=m_scales[:],
+                start=True,
+                stop=True,
+            )
 
         def finish_group(g, w_operands, m_operand):
-            m_codes, m_scales = m_operand
-            result = columns.tile([P, GROUP, O_TILES, PIXELS], F32)
-            for t in range(O_TILES):
-                w_codes, w_scales = w_operands[t]
-                acc = sums.tile([P, GROUP_COLS], F32)
-                nc.tensor.matmul_mx(
-                    out=acc[:],
-                    lhsT=w_codes[:].bitcast(FP8X4),
-                    lhsT_scale=w_scales[:],
-                    rhs=m_codes[:].bitcast(FP8X4),
-                    rhs_scale=m_scales[:],
-                    start=True,
-                    stop=True,
+            first, size = groups[g]
+            cols = size * PIXELS
+            result = columns.tile([P, size, O_TILES, PIXELS], F32)
+
+            def scalar_pass(t):
+                bank = psum.tile([P, cols], F32)
+                multiply_mx(bank[:], w_operands[t], m_operand)
+                nc.scalar.activation(
+                    out=result[:, :, t, :],
+                    in_=bank[:].rearrange("m (i w) -> m i w", w=PIXELS),
+                    func=IDENTITY,
+                    bias=bias[:, t : t + 1],
+                    scale=1.0,
                 )
-                acc_view = acc[:].rearrange("m (i w) -> m i w", w=PIXELS)
-                if g < SHARED_FROM or t % 2 == 0:
-                    nc.scalar.activation(
-                        out=result[:, :, t, :],
-                        in_=acc_view,
-                        func=mybir.ActivationFunctionType.Identity,
-                        bias=bias[:, t : t + 1],
-                        scale=1.0,
-                    )
-                else:
-                    nc.vector.tensor_scalar_add(
-                        out=result[:, :, t, :], in0=acc_view, scalar1=bias[:, t : t + 1]
-                    )
-            nc.sync.dma_start(
-                out=out_view[:, g * GROUP : (g + 1) * GROUP, :],
-                in_=result[:].rearrange("m i t w -> m i (t w)"),
-            )
+
+            def store(t_from, t_to):
+                nc.sync.dma_start(
+                    out=out_view[:, first : first + size, t_from:t_to, :],
+                    in_=result[:, :, t_from:t_to, :],
+                )
+
+            scalar_pass(0)
+            if g < SHARED_FROM:
+                scalar_pass(1)
+                if g < HALVED_BEFORE:
+                    store(0, 2)
+                scalar_pass(2)
+                scalar_pass(3)
+            else:
+                bank = psum.tile([P, 2, cols], F32)
+                for k in range(2):
+                    multiply_mx(bank[:, k, :], w_operands[2 + k], m_operand)
+                scalar_pass(1)
+                shape = [P, 2, size, PIXELS]
+                nc.vector.tensor_tensor(
+                    out=result[:, :, 2:4, :].rearrange("m i t w -> m t i w"),
+                    in0=bank[:].rearrange("m t (i w) -> m t i w", w=PIXELS),
+                    in1=bias[:, 2:4].unsqueeze(2).unsqueeze(3).to_broadcast(shape),
+                    op=mybir.AluOpType.add,
+                )
+            store(2 if g < HALVED_BEFORE else 0, O_TILES)
 
         q_cols = turn_q()
         w_grouped_all = [turn_weights(t) for t in range(O_TILES)]
-        m_grouped = multiply_q(q_cols, 0)
+        m_grouped_all = [multiply_q(q_cols, g) for g in range(3)]
         w_operands = [quantise_weights(w_grouped_all[0])]
-        m_operands = [quantise_columns(m_grouped)]
-        w_operands.extend(quantise_weights(w_grouped_all[t]) for t in range(1, O_TILES))
-        for g in range(1, GROUPS):
-            m_operands.append(quantise_columns(multiply_q(q_cols, g)))
-        for g in range(GROUPS):
+        m_operands = [quantise_columns(m_grouped_all[0], 0)]
+        w_operands.append(quantise_weights(w_grouped_all[1]))
+        m_operands.append(quantise_columns(m_grouped_all[1], 1))
+        w_operands.append(quantise_weights(w_grouped_all[2]))
+        w_operands.append(quantise_weights(w_grouped_all[3]))
+        m_grouped_all.append(multiply_q(q_cols, 3))
+        m_operands.append(quantise_columns(m_grouped_all[2], 2))
+        for g in range(4, len(groups)):
+            m_grouped_all.append(multiply_q(q_cols, g))
+            m_operands.append(quantise_columns(m_grouped_all[g - 1], g - 1))
+        m_operands.append(quantise_columns(m_grouped_all[-1], len(groups) - 1))
+        for g in range(len(groups)):
             finish_group(g, w_operands, m_operands[g])

@@ -45,10 +45,8 @@ def tile_rpn_modulator_pb_s_kernel(tc, q, feats, po_w, po_b, out):
         make_identity(nc, identity[:])
 
         q_rows = consts.tile([P, CHANNELS], BF16)
-        for k in range(2):
-            nc.sync.dma_start(
-                out=q_rows[k * ROWS : (k + 1) * ROWS, :], in_=q.rearrange("b i c -> (b i) c")
-            )
+        nc.sync.dma_start(out=q_rows[0:ROWS, :], in_=q.rearrange("b i c -> (b i) c"))
+        nc.sync.dma_start(out=q_rows[ROWS : 2 * ROWS, :], in_=po_b.partition_broadcast(ROWS))
         nc.vector.memset(q_rows[2 * ROWS : 4 * ROWS, :], 0.0)
         nc.vector.memset(q_rows[4 * ROWS : P, :], 0.0)
         feats_view = feats.rearrange("b (p j) y x -> b p (j y x)", j=PACK)
@@ -63,8 +61,6 @@ def tile_rpn_modulator_pb_s_kernel(tc, q, feats, po_w, po_b, out):
             w_rows = weights.tile([P, CHANNELS], BF16)
             nc.sync.dma_start(out=w_rows[:], in_=w_view[t])
             w_rows_all.append(w_rows)
-        bias = consts.tile([P, O_TILES], BF16)
-        nc.sync.dma_start(out=bias[:], in_=po_b.rearrange("(m t) -> m t", t=O_TILES))
 
         feats_grouped_all = []
         for b in range(IMAGES):
@@ -85,12 +81,12 @@ def tile_rpn_modulator_pb_s_kernel(tc, q, feats, po_w, po_b, out):
 
         def turn_q():
             q_turned = turn(q_rows[:])
-            q_cols = consts.tile([P, ROWS, PACK], BF16)
+            q_cols = consts.tile([P, ROWS + 1, PACK], BF16)
             nc.vector.tensor_copy(
                 out=q_cols[:].rearrange("p r j -> p (r j)").bitcast(F32).rearrange(
                     "p (r u) -> p r u", u=HALVES
                 ),
-                in_=q_turned[:, :, 0:ROWS].rearrange("p u r -> p r u"),
+                in_=q_turned[:, :, 0 : ROWS + 1].rearrange("p u r -> p r u"),
             )
             return q_cols
 
@@ -193,6 +189,7 @@ def tile_rpn_modulator_pb_s_kernel(tc, q, feats, po_w, po_b, out):
             store(2 if g < HALVED_BEFORE else 0, O_TILES)
 
         q_cols = turn_q()
+        bias = q_cols[:, ROWS, :]
         w_grouped_all = [turn_weights(t) for t in range(O_TILES)]
         m_grouped_all = [multiply_q(q_cols, g) for g in range(3)]
         w_operands = [quantise_weights(w_grouped_all[0])]

@@ -20,9 +20,8 @@ CHANNELS = 512
 PIXELS = 64
 ROWS = IMAGES * INSTANCES
 O_TILES = CHANNELS // P
-GROUP_SIZES = (2, 2, 4, 4, 2, 2)
-SHARED_FROM = 3
-HALVED_BEFORE = 1
+GROUP_SIZES = (2, 2, 2, 2, 4, 4)
+VECTOR_PAIRS = {4: (1,), 5: (1,)}
 BANKS = 8
 
 FLOPS = 2 * ROWS * PIXELS * CHANNELS * CHANNELS
@@ -51,26 +50,33 @@ def tile_rpn_modulator_pb_s_kernel(tc, q, feats, po_w, po_b, out):
         nc.vector.memset(q_rows[4 * ROWS : P, :], 0.0)
         feats_view = feats.rearrange("b (p j) y x -> b p (j y x)", j=PACK)
         feats_rows_all = []
-        for b in range(IMAGES):
+
+        def load_feats(b):
             feats_rows = images.tile([P, PACK * PIXELS], BF16)
             nc.sync.dma_start(out=feats_rows[:], in_=feats_view[b])
             feats_rows_all.append(feats_rows)
+
         w_view = po_w.rearrange("(m t) c -> t m c", t=O_TILES)
         w_rows_all = []
-        for t in range(O_TILES):
+
+        def load_weights(t):
             w_rows = weights.tile([P, CHANNELS], BF16)
             nc.sync.dma_start(out=w_rows[:], in_=w_view[t])
             w_rows_all.append(w_rows)
 
-        feats_grouped_all = []
-        for b in range(IMAGES):
+        load_weights(0)
+        load_feats(0)
+        load_weights(1)
+        load_weights(2)
+        load_weights(3)
+        load_feats(1)
+        def regroup(b):
             feats_grouped = images.tile([P, PIXELS, PACK], BF16)
-            regroup = nc.vector.tensor_copy if b == 0 else nc.scalar.copy
-            regroup(
+            nc.vector.tensor_copy(
                 out=feats_grouped[:],
                 in_=feats_rows_all[b][:].rearrange("p (j w) -> p w j", j=PACK),
             )
-            feats_grouped_all.append(feats_grouped)
+            return feats_grouped
 
         def turn(rows):
             words = rows.bitcast(F32).rearrange("r (p u) -> r u p", u=HALVES)
@@ -130,7 +136,7 @@ def tile_rpn_modulator_pb_s_kernel(tc, q, feats, po_w, po_b, out):
             )
             return w_codes, w_scales
 
-        out_view = out.rearrange("b i (m t) y x -> m (b i) t (y x)", t=O_TILES)
+        out_view = out.rearrange("b i (m t) y x -> m (b i) (t y x)", t=O_TILES)
 
         def multiply_mx(acc, w_operand, m_operand):
             w_codes, w_scales = w_operand
@@ -161,48 +167,46 @@ def tile_rpn_modulator_pb_s_kernel(tc, q, feats, po_w, po_b, out):
                     scale=1.0,
                 )
 
-            def store(t_from, t_to):
-                nc.sync.dma_start(
-                    out=out_view[:, first : first + size, t_from:t_to, :],
-                    in_=result[:, :, t_from:t_to, :],
-                )
-
-            scalar_pass(0)
-            if g < SHARED_FROM:
-                scalar_pass(1)
-                if g < HALVED_BEFORE:
-                    store(0, 2)
-                scalar_pass(2)
-                scalar_pass(3)
-            else:
+            def vector_pair(t):
                 bank = psum.tile([P, 2, cols], F32)
                 for k in range(2):
-                    multiply_mx(bank[:, k, :], w_operands[2 + k], m_operand)
-                scalar_pass(1)
+                    multiply_mx(bank[:, k, :], w_operands[t + k], m_operand)
                 shape = [P, 2, size, PIXELS]
                 nc.vector.tensor_tensor(
-                    out=result[:, :, 2:4, :].rearrange("m i t w -> m t i w"),
+                    out=result[:, :, t : t + 2, :].rearrange("m i t w -> m t i w"),
                     in0=bank[:].rearrange("m t (i w) -> m t i w", w=PIXELS),
-                    in1=bias[:, 2:4].unsqueeze(2).unsqueeze(3).to_broadcast(shape),
+                    in1=bias[:, t : t + 2].unsqueeze(2).unsqueeze(3).to_broadcast(shape),
                     op=mybir.AluOpType.add,
                 )
-            store(2 if g < HALVED_BEFORE else 0, O_TILES)
 
+            for pair in range(2):
+                if pair in VECTOR_PAIRS.get(g, ()):
+                    vector_pair(2 * pair)
+                else:
+                    scalar_pass(2 * pair)
+                    scalar_pass(2 * pair + 1)
+            nc.sync.dma_start(
+                out=out_view[:, first : first + size, :],
+                in_=result[:].rearrange("m i t w -> m i (t w)"),
+            )
+
+        feats_grouped_all = [regroup(0)]
         q_cols = turn_q()
         bias = q_cols[:, ROWS, :]
         w_grouped_all = [turn_weights(t) for t in range(O_TILES)]
-        m_grouped_all = [multiply_q(q_cols, g) for g in range(3)]
+        m_grouped_all = [multiply_q(q_cols, g) for g in range(2)]
         w_operands = [quantise_weights(w_grouped_all[0])]
         m_operands = [quantise_columns(m_grouped_all[0], 0)]
         w_operands.append(quantise_weights(w_grouped_all[1]))
         m_operands.append(quantise_columns(m_grouped_all[1], 1))
         w_operands.append(quantise_weights(w_grouped_all[2]))
         w_operands.append(quantise_weights(w_grouped_all[3]))
+        m_grouped_all.append(multiply_q(q_cols, 2))
         m_grouped_all.append(multiply_q(q_cols, 3))
         m_operands.append(quantise_columns(m_grouped_all[2], 2))
+        feats_grouped_all.append(regroup(1))
+        m_operands.append(quantise_columns(m_grouped_all[3], 3))
         for g in range(4, len(groups)):
-            m_grouped_all.append(multiply_q(q_cols, g))
-            m_operands.append(quantise_columns(m_grouped_all[g - 1], g - 1))
-        m_operands.append(quantise_columns(m_grouped_all[-1], len(groups) - 1))
+            m_operands.append(quantise_columns(multiply_q(q_cols, g), g))
         for g in range(len(groups)):
             finish_group(g, w_operands, m_operands[g])

@@ -20,8 +20,12 @@ CHANNELS = 512
 PIXELS = 64
 ROWS = IMAGES * INSTANCES
 O_TILES = CHANNELS // P
-GROUP_SIZES = (2, 2, 2, 2, 4, 4)
-VECTOR_PAIRS = {4: (1,), 5: (1,)}
+GROUP = 2
+GROUPS = ROWS // GROUP
+GROUP_COLS = GROUP * PIXELS
+BLOCK = 4
+BLOCKS = ROWS // BLOCK
+SHARED_FROM = 3
 BANKS = 8
 
 FLOPS = 2 * ROWS * PIXELS * CHANNELS * CHANNELS
@@ -29,14 +33,12 @@ FLOPS = 2 * ROWS * PIXELS * CHANNELS * CHANNELS
 
 def tile_rpn_modulator_pb_s_kernel(tc, q, feats, po_w, po_b, out):
     nc = tc.nc
-    groups = []
-    for size in GROUP_SIZES:
-        groups.append((sum(GROUP_SIZES[: len(groups)]), size))
     with ExitStack() as ctx:
         consts = ctx.enter_context(tc.tile_pool(name="consts", bufs=1))
         images = ctx.enter_context(tc.tile_pool(name="images", bufs=IMAGES))
         weights = ctx.enter_context(tc.tile_pool(name="weights", bufs=O_TILES))
-        columns = ctx.enter_context(tc.tile_pool(name="columns", bufs=len(GROUP_SIZES)))
+        blocks = ctx.enter_context(tc.tile_pool(name="blocks", bufs=BLOCKS))
+        columns = ctx.enter_context(tc.tile_pool(name="columns", bufs=GROUPS))
         psum = ctx.enter_context(tc.psum_pool(name="psum", bufs=BANKS))
         ctx.enter_context(tc.manual_schedule())
 
@@ -64,15 +66,15 @@ def tile_rpn_modulator_pb_s_kernel(tc, q, feats, po_w, po_b, out):
             nc.sync.dma_start(out=w_rows[:], in_=w_view[t])
             w_rows_all.append(w_rows)
 
-        load_weights(0)
         load_feats(0)
+        load_weights(0)
+        load_feats(1)
         load_weights(1)
         load_weights(2)
         load_weights(3)
-        load_feats(1)
-        def regroup(b):
+        def regroup(b, copy):
             feats_grouped = images.tile([P, PIXELS, PACK], BF16)
-            nc.vector.tensor_copy(
+            copy(
                 out=feats_grouped[:],
                 in_=feats_rows_all[b][:].rearrange("p (j w) -> p w j", j=PACK),
             )
@@ -96,26 +98,28 @@ def tile_rpn_modulator_pb_s_kernel(tc, q, feats, po_w, po_b, out):
             )
             return q_cols
 
-        def multiply_q(q_cols, g):
-            first, size = groups[g]
-            shape = [P, size, PIXELS, PACK]
-            m_grouped = columns.tile(shape, BF16, align_bytes=64)
+        def multiply_q(q_cols, b):
+            shape = [P, INSTANCES, PIXELS, PACK]
+            m_grouped = images.tile(shape, BF16, align_bytes=64)
+            rows = slice(b * INSTANCES, (b + 1) * INSTANCES)
             nc.vector.tensor_tensor(
                 out=m_grouped[:],
-                in0=feats_grouped_all[first // INSTANCES][:].unsqueeze(1).to_broadcast(shape),
-                in1=q_cols[:, first : first + size, :].unsqueeze(2).to_broadcast(shape),
+                in0=feats_grouped_all[b][:].unsqueeze(1).to_broadcast(shape),
+                in1=q_cols[:, rows, :].unsqueeze(2).to_broadcast(shape),
                 op=mybir.AluOpType.mult,
             )
             return m_grouped
 
-        def quantise_columns(m_grouped, g):
-            cols = groups[g][1] * PIXELS
-            m_codes = columns.tile([P, cols], U32, align_bytes=64)
-            m_scales = columns.tile([P, cols], U8, align_bytes=64)
+        def quantise_columns(m_grouped_all, k):
+            first = k * BLOCK % INSTANCES
+            m_codes = blocks.tile([P, BLOCK * PIXELS], U32, align_bytes=64)
+            m_scales = blocks.tile([P, BLOCK * PIXELS], U8, align_bytes=64)
             nc.vector.quantize_mx(
                 out=m_codes[:].bitcast(FP8X4),
                 scales=m_scales[:],
-                in_=m_grouped[:].rearrange("p i w j -> p (i w j)"),
+                in_=m_grouped_all[k * BLOCK // INSTANCES][:, first : first + BLOCK].rearrange(
+                    "p i w j -> p (i w j)"
+                ),
             )
             return m_codes, m_scales
 
@@ -138,27 +142,27 @@ def tile_rpn_modulator_pb_s_kernel(tc, q, feats, po_w, po_b, out):
 
         out_view = out.rearrange("b i (m t) y x -> m (b i) (t y x)", t=O_TILES)
 
-        def multiply_mx(acc, w_operand, m_operand):
-            w_codes, w_scales = w_operand
-            m_codes, m_scales = m_operand
-            nc.tensor.matmul_mx(
-                out=acc,
-                lhsT=w_codes[:].bitcast(FP8X4),
-                lhsT_scale=w_scales[:],
-                rhs=m_codes[:].bitcast(FP8X4),
-                rhs_scale=m_scales[:],
-                start=True,
-                stop=True,
-            )
+        def finish_group(g, w_operands, m_operands):
+            m_codes, m_scales = m_operands[g * GROUP // BLOCK]
+            start_col = g * GROUP_COLS % (BLOCK * PIXELS)
+            cols = slice(start_col, start_col + GROUP_COLS)
+            result = columns.tile([P, GROUP, O_TILES, PIXELS], F32)
 
-        def finish_group(g, w_operands, m_operand):
-            first, size = groups[g]
-            cols = size * PIXELS
-            result = columns.tile([P, size, O_TILES, PIXELS], F32)
+            def multiply_mx(acc, t):
+                w_codes, w_scales = w_operands[t]
+                nc.tensor.matmul_mx(
+                    out=acc,
+                    lhsT=w_codes[:].bitcast(FP8X4),
+                    lhsT_scale=w_scales[:],
+                    rhs=m_codes[:, cols].bitcast(FP8X4),
+                    rhs_scale=m_scales[:, cols],
+                    start=True,
+                    stop=True,
+                )
 
             def scalar_pass(t):
-                bank = psum.tile([P, cols], F32)
-                multiply_mx(bank[:], w_operands[t], m_operand)
+                bank = psum.tile([P, GROUP_COLS], F32)
+                multiply_mx(bank[:], t)
                 nc.scalar.activation(
                     out=result[:, :, t, :],
                     in_=bank[:].rearrange("m (i w) -> m i w", w=PIXELS),
@@ -168,45 +172,44 @@ def tile_rpn_modulator_pb_s_kernel(tc, q, feats, po_w, po_b, out):
                 )
 
             def vector_pair(t):
-                bank = psum.tile([P, 2, cols], F32)
+                bank = psum.tile([P, 2, GROUP_COLS], F32)
                 for k in range(2):
-                    multiply_mx(bank[:, k, :], w_operands[t + k], m_operand)
-                shape = [P, 2, size, PIXELS]
+                    multiply_mx(bank[:, k, :], t + k)
                 nc.vector.tensor_tensor(
                     out=result[:, :, t : t + 2, :].rearrange("m i t w -> m t i w"),
                     in0=bank[:].rearrange("m t (i w) -> m t i w", w=PIXELS),
-                    in1=bias[:, t : t + 2].unsqueeze(2).unsqueeze(3).to_broadcast(shape),
+                    in1=bias[:, t : t + 2]
+                    .unsqueeze(2)
+                    .unsqueeze(3)
+                    .to_broadcast([P, 2, GROUP, PIXELS]),
                     op=mybir.AluOpType.add,
                 )
 
-            for pair in range(2):
-                if pair in VECTOR_PAIRS.get(g, ()):
-                    vector_pair(2 * pair)
-                else:
-                    scalar_pass(2 * pair)
-                    scalar_pass(2 * pair + 1)
+            scalar_pass(0)
+            if g < SHARED_FROM:
+                scalar_pass(1)
+                scalar_pass(2)
+                scalar_pass(3)
+            else:
+                vector_pair(2)
+                scalar_pass(1)
             nc.sync.dma_start(
-                out=out_view[:, first : first + size, :],
+                out=out_view[:, g * GROUP : (g + 1) * GROUP, :],
                 in_=result[:].rearrange("m i t w -> m i (t w)"),
             )
 
-        feats_grouped_all = [regroup(0)]
+        feats_grouped_all = [regroup(0, nc.vector.tensor_copy), regroup(1, nc.scalar.copy)]
         q_cols = turn_q()
         bias = q_cols[:, ROWS, :]
         w_grouped_all = [turn_weights(t) for t in range(O_TILES)]
-        m_grouped_all = [multiply_q(q_cols, g) for g in range(2)]
+        m_grouped_all = [multiply_q(q_cols, 0)]
         w_operands = [quantise_weights(w_grouped_all[0])]
-        m_operands = [quantise_columns(m_grouped_all[0], 0)]
-        w_operands.append(quantise_weights(w_grouped_all[1]))
-        m_operands.append(quantise_columns(m_grouped_all[1], 1))
-        w_operands.append(quantise_weights(w_grouped_all[2]))
-        w_operands.append(quantise_weights(w_grouped_all[3]))
-        m_grouped_all.append(multiply_q(q_cols, 2))
-        m_grouped_all.append(multiply_q(q_cols, 3))
-        m_operands.append(quantise_columns(m_grouped_all[2], 2))
-        feats_grouped_all.append(regroup(1))
-        m_operands.append(quantise_columns(m_grouped_all[3], 3))
-        for g in range(4, len(groups)):
-            m_operands.append(quantise_columns(multiply_q(q_cols, g), g))
-        for g in range(len(groups)):
-            finish_group(g, w_operands, m_operands[g])
+        m_operands = [quantise_columns(m_grouped_all, 0)]
+        for t in range(1, O_TILES):
+            w_operands.append(quantise_weights(w_grouped_all[t]))
+        m_operands.append(quantise_columns(m_grouped_all, 1))
+        m_grouped_all.append(multiply_q(q_cols, 1))
+        m_operands.append(quantise_columns(m_grouped_all, 2))
+        m_operands.append(quantise_columns(m_grouped_all, 3))
+        for g in range(GROUPS):
+            finish_group(g, w_operands, m_operands)

from contextlib import ExitStack

import concourse.mybir as mybir
from concourse.masks import make_identity

F32 = mybir.dt.float32
BF16 = mybir.dt.bfloat16
U32 = mybir.dt.uint32
U8 = mybir.dt.uint8
FP8X4 = mybir.dt.float8_e4m3fn_x4
IDENTITY = mybir.ActivationFunctionType.Identity

P = 128
PACK = 4
HALVES = 2

IMAGES = 2
INSTANCES = 8
CHANNELS = 512
PIXELS = 64
ROWS = IMAGES * INSTANCES
O_TILES = CHANNELS // P
GROUP = 2
GROUPS = ROWS // GROUP
GROUP_COLS = GROUP * PIXELS
BLOCK = 4
BLOCKS = ROWS // BLOCK
SHARED_FROM = 3
BANKS = 8

FLOPS = 2 * ROWS * PIXELS * CHANNELS * CHANNELS


def tile_rpn_modulator_pb_s_kernel(tc, q, feats, po_w, po_b, out):
    nc = tc.nc
    with ExitStack() as ctx:
        consts = ctx.enter_context(tc.tile_pool(name="consts", bufs=1))
        images = ctx.enter_context(tc.tile_pool(name="images", bufs=IMAGES))
        weights = ctx.enter_context(tc.tile_pool(name="weights", bufs=O_TILES))
        blocks = ctx.enter_context(tc.tile_pool(name="blocks", bufs=BLOCKS))
        columns = ctx.enter_context(tc.tile_pool(name="columns", bufs=GROUPS))
        psum = ctx.enter_context(tc.psum_pool(name="psum", bufs=BANKS))
        ctx.enter_context(tc.manual_schedule())

        identity = consts.tile([P, P], F32)
        make_identity(nc, identity[:])

        q_rows = consts.tile([P, CHANNELS], BF16)
        nc.sync.dma_start(out=q_rows[0:ROWS, :], in_=q.rearrange("b i c -> (b i) c"))
        nc.sync.dma_start(out=q_rows[ROWS : 2 * ROWS, :], in_=po_b.partition_broadcast(ROWS))
        nc.vector.memset(q_rows[2 * ROWS : 4 * ROWS, :], 0.0)
        nc.vector.memset(q_rows[4 * ROWS : P, :], 0.0)
        feats_view = feats.rearrange("b (p j) y x -> b p (j y x)", j=PACK)
        feats_rows_all = []

        def load_feats(b):
            feats_rows = images.tile([P, PACK * PIXELS], BF16)
            nc.sync.dma_start(out=feats_rows[:], in_=feats_view[b])
            feats_rows_all.append(feats_rows)

        w_view = po_w.rearrange("(m t) c -> t m c", t=O_TILES)
        w_rows_all = []

        def load_weights(t):
            w_rows = weights.tile([P, CHANNELS], BF16)
            nc.sync.dma_start(out=w_rows[:], in_=w_view[t])
            w_rows_all.append(w_rows)

        load_feats(0)
        load_weights(0)
        load_feats(1)
        load_weights(1)
        load_weights(2)
        load_weights(3)
        def regroup(b, copy):
            feats_grouped = images.tile([P, PIXELS, PACK], BF16)
            copy(
                out=feats_grouped[:],
                in_=feats_rows_all[b][:].rearrange("p (j w) -> p w j", j=PACK),
            )
            return feats_grouped

        def turn(rows):
            words = rows.bitcast(F32).rearrange("r (p u) -> r u p", u=HALVES)
            bank = psum.tile([P, HALVES, P], F32)
            for u in range(HALVES):
                nc.tensor.transpose(bank[:, u, :], words[:, u, :], identity[:])
            return bank

        def turn_q():
            q_turned = turn(q_rows[:])
            q_cols = consts.tile([P, ROWS + 1, PACK], BF16)
            nc.vector.tensor_copy(
                out=q_cols[:].rearrange("p r j -> p (r j)").bitcast(F32).rearrange(
                    "p (r u) -> p r u", u=HALVES
                ),
                in_=q_turned[:, :, 0 : ROWS + 1].rearrange("p u r -> p r u"),
            )
            return q_cols

        def multiply_q(q_cols, b):
            shape = [P, INSTANCES, PIXELS, PACK]
            m_grouped = images.tile(shape, BF16, align_bytes=64)
            rows = slice(b * INSTANCES, (b + 1) * INSTANCES)
            nc.vector.tensor_tensor(
                out=m_grouped[:],
                in0=feats_grouped_all[b][:].unsqueeze(1).to_broadcast(shape),
                in1=q_cols[:, rows, :].unsqueeze(2).to_broadcast(shape),
                op=mybir.AluOpType.mult,
            )
            return m_grouped

        def quantise_columns(m_grouped_all, k):
            first = k * BLOCK % INSTANCES
            m_codes = blocks.tile([P, BLOCK * PIXELS], U32, align_bytes=64)
            m_scales = blocks.tile([P, BLOCK * PIXELS], U8, align_bytes=64)
            nc.vector.quantize_mx(
                out=m_codes[:].bitcast(FP8X4),
                scales=m_scales[:],
                in_=m_grouped_all[k * BLOCK // INSTANCES][:, first : first + BLOCK].rearrange(
                    "p i w j -> p (i w j)"
                ),
            )
            return m_codes, m_scales

        def turn_weights(t):
            w_turned = turn(w_rows_all[t][:])
            w_grouped = weights.tile([P, P * PACK], BF16, align_bytes=64)
            nc.scalar.copy(
                out=w_grouped[:].bitcast(F32).rearrange("p (m u) -> p m u", u=HALVES),
                in_=w_turned[:].rearrange("p u m -> p m u"),
            )
            return w_grouped

        def quantise_weights(w_grouped):
            w_codes = weights.tile([P, P], U32, align_bytes=64)
            w_scales = weights.tile([P, P], U8, align_bytes=64)
            nc.vector.quantize_mx(
                out=w_codes[:].bitcast(FP8X4), scales=w_scales[:], in_=w_grouped[:]
            )
            return w_codes, w_scales

        out_view = out.rearrange("b i (m t) y x -> m (b i) (t y x)", t=O_TILES)

        def finish_group(g, w_operands, m_operands):
            m_codes, m_scales = m_operands[g * GROUP // BLOCK]
            start_col = g * GROUP_COLS % (BLOCK * PIXELS)
            cols = slice(start_col, start_col + GROUP_COLS)
            result = columns.tile([P, GROUP, O_TILES, PIXELS], F32)

            def multiply_mx(acc, t):
                w_codes, w_scales = w_operands[t]
                nc.tensor.matmul_mx(
                    out=acc,
                    lhsT=w_codes[:].bitcast(FP8X4),
                    lhsT_scale=w_scales[:],
                    rhs=m_codes[:, cols].bitcast(FP8X4),
                    rhs_scale=m_scales[:, cols],
                    start=True,
                    stop=True,
                )

            def scalar_pass(t):
                bank = psum.tile([P, GROUP_COLS], F32)
                multiply_mx(bank[:], t)
                nc.scalar.activation(
                    out=result[:, :, t, :],
                    in_=bank[:].rearrange("m (i w) -> m i w", w=PIXELS),
                    func=IDENTITY,
                    bias=bias[:, t : t + 1],
                    scale=1.0,
                )

            def vector_pair(t):
                bank = psum.tile([P, 2, GROUP_COLS], F32)
                for k in range(2):
                    multiply_mx(bank[:, k, :], t + k)
                nc.vector.tensor_tensor(
                    out=result[:, :, t : t + 2, :].rearrange("m i t w -> m t i w"),
                    in0=bank[:].rearrange("m t (i w) -> m t i w", w=PIXELS),
                    in1=bias[:, t : t + 2]
                    .unsqueeze(2)
                    .unsqueeze(3)
                    .to_broadcast([P, 2, GROUP, PIXELS]),
                    op=mybir.AluOpType.add,
                )

            scalar_pass(0)
            if g < SHARED_FROM:
                scalar_pass(1)
                scalar_pass(2)
                scalar_pass(3)
            else:
                vector_pair(2)
                scalar_pass(1)
            nc.sync.dma_start(
                out=out_view[:, g * GROUP : (g + 1) * GROUP, :],
                in_=result[:].rearrange("m i t w -> m i (t w)"),
            )

        feats_grouped_all = [regroup(0, nc.vector.tensor_copy), regroup(1, nc.scalar.copy)]
        q_cols = turn_q()
        bias = q_cols[:, ROWS, :]
        w_grouped_all = [turn_weights(t) for t in range(O_TILES)]
        m_grouped_all = [multiply_q(q_cols, 0)]
        w_operands = [quantise_weights(w_grouped_all[0])]
        m_operands = [quantise_columns(m_grouped_all, 0)]
        for t in range(1, O_TILES):
            w_operands.append(quantise_weights(w_grouped_all[t]))
        m_operands.append(quantise_columns(m_grouped_all, 1))
        m_grouped_all.append(multiply_q(q_cols, 1))
        m_operands.append(quantise_columns(m_grouped_all, 2))
        m_operands.append(quantise_columns(m_grouped_all, 3))
        for g in range(GROUPS):
            finish_group(g, w_operands, m_operands)
